import numpy as np
import ml_dtypes


def mxq(x, axis, fmt="e4m3"):
    dtype, down = {"e4m3": (ml_dtypes.float8_e4m3fn, 7), "e5m2": (ml_dtypes.float8_e5m2, 14)}[fmt]
    v = np.moveaxis(np.asarray(x, np.float32).astype(ml_dtypes.bfloat16).astype(np.float64), axis, -1)
    blocks = v.reshape(v.shape[:-1] + (-1, 32))
    amax = np.abs(blocks).max(-1, keepdims=True)
    byte = np.maximum(np.where(amax > 0, np.frexp(amax)[1] - 1 + 127, 0) - down, 1)
    scale = np.exp2(byte - 127.0)
    codes = (blocks / scale).astype(np.float32).astype(dtype).astype(np.float64)
    return np.moveaxis((codes * scale).reshape(v.shape), -1, axis)


WIDE = False


def mx_kscale(k):
    if not WIDE:
        return np.ones(k)
    levels = np.array([10, -10, 5, -5, 0])
    a = np.random.permutation(np.resize(levels, k // 512 * 4)).reshape(k // 512, 4)
    idx = np.arange(k)
    return np.exp2(a[idx // 512, idx % 128 // 32])


BF16 = ml_dtypes.bfloat16


def bf(x):
    return np.asarray(x, np.float32).astype(BF16)


def f64(x):
    return np.asarray(x).astype(np.float64)


B, N, DIN, DH, DOUT = 1536, 4, 512, 512, 512
EPS = 1e-5


def elu(v):
    return np.where(v > 0.0, v, np.expm1(np.minimum(v, 0.0)))


def sigmoid(v):
    return 1.0 / (1.0 + np.exp(-v))


def setup_inputs():
    rn = np.random.standard_normal
    s, t = mx_kscale(DH), mx_kscale(DOUT)
    z = rn((B, N, DOUT))
    e = np.exp(z - z.max(1, keepdims=True))
    return {
        "hv": bf(elu(rn((B, N, DH))) * s),
        "x": bf(rn((B, N, DIN)) + 0.5),
        "sel_w": bf(e / e.sum(1, keepdims=True)),
        "vW1": bf(rn((N, DH, DOUT)) * 1.2 / np.sqrt(DH) / s[:, None] * t),
        "vb1": bf(rn((N, DOUT)) * 0.3 * t),
        "vW4": bf(rn((N, DOUT, DOUT)) / np.sqrt(DOUT) / t[:, None]),
        "vb4": bf(rn((N, DOUT)) * 0.3),
        "vW5": bf(rn((N, DOUT, DOUT)) / np.sqrt(DOUT) / t[:, None]),
        "vb5": bf(rn((N, DOUT)) * 0.3),
        "vlng": bf(1.0 + 0.2 * rn((N, DOUT))),
        "vlnb": bf(0.2 * rn((N, DOUT))),
    }


def reference(hv, x, sel_w, vW1, vb1, vW4, vb4, vW5, vb5, vlng, vlnb):
    hq = mxq(f64(hv).transpose(1, 0, 2), 2, "e4m3")
    e1v = (hq @ mxq(f64(vW1), 1, "e4m3")) + f64(vb1)[:, None, :]
    eq = mxq(e1v, 2, "e4m3")
    gv = sigmoid((eq @ mxq(f64(vW4), 1, "e4m3")) + f64(vb4)[:, None, :]) * ((eq @ mxq(f64(vW5), 1, "e4m3")) + f64(vb5)[:, None, :])
    r = f64(x) + gv.transpose(1, 0, 2)
    yv = (r - r.mean(-1, keepdims=True)) * (1.0 / np.sqrt(r.var(-1, keepdims=True) + EPS)) * f64(vlng) + f64(vlnb)
    return np.sum(f64(sel_w) * yv, axis=1)

@@ -1,0 +1,271 @@
+from contextlib import ExitStack
+
+import concourse.mybir as mybir
+from concourse.masks import make_identity
+
+F32 = mybir.dt.float32
+BF16 = mybir.dt.bfloat16
+U32 = mybir.dt.uint32
+U8 = mybir.dt.uint8
+FP8X4 = mybir.dt.float8_e4m3fn_x4
+ALU = mybir.AluOpType
+ACT = mybir.ActivationFunctionType
+
+P = 128
+PACK = 4
+BATCH = 1536
+VARS = 4
+D = 512
+CHUNKS = D // P
+UNIT_ROWS = 512
+UNIT_TILES = UNIT_ROWS // P
+UNITS = BATCH // UNIT_ROWS
+EPS = 1e-5
+
+FLOPS = 3 * VARS * 2 * BATCH * D * D
+
+
+def tile_variableselectionnetwork_pb_t_kernel(
+    tc, hv, x, sel_w, vW1, vb1, vW4, vb4, vW5, vb5, vlng, vlnb, out
+):
+    nc = tc.nc
+    with ExitStack() as ctx:
+        const = ctx.enter_context(tc.tile_pool(name="const", bufs=1))
+        wstage = ctx.enter_context(tc.tile_pool(name="wstage", bufs=2))
+        wquant = ctx.enter_context(tc.tile_pool(name="wquant", bufs=2))
+        loads = ctx.enter_context(tc.tile_pool(name="loads", bufs=3))
+        quant = ctx.enter_context(tc.tile_pool(name="quant", bufs=2))
+        gate = ctx.enter_context(tc.tile_pool(name="gate", bufs=2))
+        norm = ctx.enter_context(tc.tile_pool(name="norm", bufs=8))
+        stat = ctx.enter_context(tc.tile_pool(name="stat", bufs=3))
+        psum = ctx.enter_context(tc.psum_pool(name="psum", bufs=1))
+
+        ident_f = const.tile([P, P], F32)
+        make_identity(nc, ident_f[:])
+        ident_b = const.tile([P, P], BF16)
+        make_identity(nc, ident_b[:])
+        neg_half = const.tile([P, UNIT_TILES], F32)
+        nc.vector.memset(neg_half[:], -0.5)
+
+        bias_rows = const.tile([P, P], BF16)
+        nc.vector.memset(bias_rows[:], 0.0)
+        for k, vec in enumerate((vb1, vb4, vb5)):
+            nc.sync.dma_start(
+                out=bias_rows[k * VARS * CHUNKS : (k + 1) * VARS * CHUNKS, :],
+                in_=vec.rearrange("n (c m) -> (n c) m", m=P),
+            )
+        bias_ps = psum.tile([P, P], BF16, tag="hv_t")
+        nc.tensor.transpose(bias_ps[:], bias_rows[:], ident_b[:])
+        bias_cols = const.tile([P, 3, VARS, CHUNKS], F32)
+        nc.vector.tensor_copy(
+            out=bias_cols[:].rearrange("p k n c -> p (k n c)"), in_=bias_ps[:, 0 : 3 * VARS * CHUNKS]
+        )
+
+        gain = const.tile([P, VARS, D], BF16)
+        shift = const.tile([P, VARS, D], BF16)
+
+        acc = const.tile([P, BATCH // P, D], F32)
+
+        def quantise_weight(dram_view, raw_view_pattern, tag):
+            raw = wstage.tile([P, PACK, D], BF16, tag="w_raw", bufs=3)
+            if raw_view_pattern is None:
+                nc.sync.dma_start(out=raw[:], in_=dram_view)
+            else:
+                nc.sync.dma_start(out=raw[:].rearrange(raw_view_pattern, u=2), in_=dram_view)
+            grouped = wstage.tile([P, D, PACK], BF16, tag="w_grp", align_bytes=64)
+            nc.scalar.copy(
+                out=grouped[:].rearrange("p (c i) t -> p c t i", i=4),
+                in_=raw[:].rearrange("p t (c i) -> p c t i", i=4),
+            )
+            codes = wquant.tile([P, D], U32, tag=tag + "_codes", align_bytes=64)
+            scales = wquant.tile([P, D], U8, tag=tag + "_scales", align_bytes=64)
+            nc.vector.quantize_mx(
+                out=codes[:].bitcast(FP8X4),
+                scales=scales[:],
+                in_=grouped[:].rearrange("p c t -> p (c t)"),
+            )
+            return codes, scales
+
+        for n in range(VARS):
+            w1_codes, w1_scales = quantise_weight(
+                vW1[n].rearrange("(u p e) c -> p u e c", u=2, e=2), "p (u e) c -> p u e c", "w1"
+            )
+            w4_codes, w4_scales = quantise_weight(vW4[n].rearrange("(t p) c -> p t c", p=P), None, "w4")
+            w5_codes, w5_scales = quantise_weight(vW5[n].rearrange("(t p) c -> p t c", p=P), None, "w5")
+            if n == 0:
+                nc.sync.dma_start(
+                    out=gain[:].rearrange("p n d -> p (n d)"),
+                    in_=vlng.rearrange("n d -> (n d)").partition_broadcast(P),
+                )
+                nc.sync.dma_start(
+                    out=shift[:].rearrange("p n d -> p (n d)"),
+                    in_=vlnb.rearrange("n d -> (n d)").partition_broadcast(P),
+                )
+
+            for unit in range(UNITS):
+                rows = slice(unit * UNIT_ROWS, (unit + 1) * UNIT_ROWS)
+                hv_u = loads.tile([P, UNIT_TILES * D], BF16, tag="hv_u")
+                nc.sync.dma_start(
+                    out=hv_u[:].rearrange("p (i d) -> p i d", i=UNIT_TILES),
+                    in_=hv[rows, n, :].rearrange("(i p) d -> p i d", p=P),
+                )
+                x_u = loads.tile([P, UNIT_TILES, D], BF16, tag="x_u")
+                nc.sync.dma_start(out=x_u[:], in_=x[rows, n, :].rearrange("(i p) d -> p i d", p=P))
+                sel_u = loads.tile([P, UNIT_TILES, D], BF16, tag="sel_u")
+                nc.sync.dma_start(out=sel_u[:], in_=sel_w[rows, n, :].rearrange("(i p) d -> p i d", p=P))
+
+                hv_words = hv_u[:].bitcast(F32)
+                hv_grp = quant.tile([P, UNIT_ROWS * PACK], BF16, tag="hv_grp", align_bytes=64)
+                hv_grp_words = hv_grp[:].bitcast(F32).rearrange("p (b u) -> p b u", u=2)
+                for half in range(2):
+                    hv_t = psum.tile([P, 2, 2 * P], F32, tag="hv_t")
+                    for u in range(2):
+                        for k in range(2):
+                            i = 2 * half + k
+                            nc.tensor.transpose(
+                                hv_t[:, u, k * P : (k + 1) * P],
+                                hv_words[:, i * 2 * P + u * P : i * 2 * P + (u + 1) * P],
+                                ident_f[:],
+                            )
+                    nc.scalar.copy(
+                        out=hv_grp_words[:, half * 2 * P : (half + 1) * 2 * P, :],
+                        in_=hv_t[:].rearrange("p u b -> p b u"),
+                    )
+                hv_codes = quant.tile([P, UNIT_ROWS], U32, tag="hv_codes", align_bytes=64)
+                hv_scales = quant.tile([P, UNIT_ROWS], U8, tag="hv_scales", align_bytes=64)
+                nc.vector.quantize_mx(out=hv_codes[:].bitcast(FP8X4), scales=hv_scales[:], in_=hv_grp[:])
+
+                e1_grp = quant.tile([P, UNIT_ROWS, PACK], BF16, tag="e1_grp", align_bytes=64)
+                for i in range(UNIT_TILES):
+                    cols = slice(i * P, (i + 1) * P)
+                    e1_ps = psum.tile([P, CHUNKS, P], F32, tag="e1_ps", bufs=2)
+                    for c in range(CHUNKS):
+                        nc.tensor.matmul_mx(
+                            out=e1_ps[:, c, :],
+                            lhsT=w1_codes[:, c * P : (c + 1) * P].bitcast(FP8X4),
+                            lhsT_scale=w1_scales[:, c * P : (c + 1) * P],
+                            rhs=hv_codes[:, cols].bitcast(FP8X4),
+                            rhs_scale=hv_scales[:, cols],
+                            start=True,
+                            stop=True,
+                        )
+                    nc.vector.tensor_tensor(
+                        out=e1_grp[:, cols, :],
+                        in0=e1_ps[:].rearrange("p c b -> p b c"),
+                        in1=bias_cols[:, 0, n, :].unsqueeze(1).to_broadcast([P, P, CHUNKS]),
+                        op=ALU.add,
+                    )
+                e1_codes = quant.tile([P, UNIT_ROWS], U32, tag="e1_codes", align_bytes=64)
+                e1_scales = quant.tile([P, UNIT_ROWS], U8, tag="e1_scales", align_bytes=64)
+                nc.vector.quantize_mx(
+                    out=e1_codes[:].bitcast(FP8X4),
+                    scales=e1_scales[:],
+                    in_=e1_grp[:].rearrange("p b t -> p (b t)"),
+                )
+
+                gv_t = gate.tile([P, CHUNKS, UNIT_ROWS], F32, tag="gv_t")
+                for c in range(CHUNKS):
+                    feats = slice(c * P, (c + 1) * P)
+                    g4_ps = psum.tile([P, UNIT_ROWS], F32, tag="g4_ps")
+                    nc.tensor.matmul_mx(
+                        out=g4_ps[:],
+                        lhsT=w4_codes[:, feats].bitcast(FP8X4),
+                        lhsT_scale=w4_scales[:, feats],
+                        rhs=e1_codes[:].bitcast(FP8X4),
+                        rhs_scale=e1_scales[:],
+                        start=True,
+                        stop=True,
+                    )
+                    g5_ps = psum.tile([P, UNIT_ROWS], F32, tag="g5_ps", bufs=2)
+                    nc.tensor.matmul_mx(
+                        out=g5_ps[:],
+                        lhsT=w5_codes[:, feats].bitcast(FP8X4),
+                        lhsT_scale=w5_scales[:, feats],
+                        rhs=e1_codes[:].bitcast(FP8X4),
+                        rhs_scale=e1_scales[:],
+                        start=True,
+                        stop=True,
+                    )
+                    sig = gate.tile([P, UNIT_ROWS], F32, tag="sig", bufs=3)
+                    nc.scalar.activation(
+                        out=sig[:], in_=g4_ps[:], func=ACT.Sigmoid, bias=bias_cols[:, 1, n, c : c + 1], scale=1.0
+                    )
+                    nc.vector.scalar_tensor_tensor(
+                        out=gv_t[:, c, :],
+                        in0=g5_ps[:],
+                        scalar=bias_cols[:, 2, n, c : c + 1],
+                        in1=sig[:],
+                        op0=ALU.add,
+                        op1=ALU.mult,
+                    )
+
+                row_sum = stat.tile([P, UNIT_TILES], F32, tag="row_sum")
+                res = []
+                for i in range(UNIT_TILES):
+                    gv_ps = psum.tile([P, D], F32, tag="gv_ps", bufs=2)
+                    for c in range(CHUNKS):
+                        nc.tensor.transpose(
+                            gv_ps[:, c * P : (c + 1) * P], gv_t[:, c, i * P : (i + 1) * P], ident_f[:]
+                        )
+                    r = norm.tile([P, D], F32, tag="r")
+                    nc.vector.scalar_tensor_tensor(
+                        out=r[:],
+                        in0=gv_ps[:],
+                        scalar=1.0,
+                        in1=x_u[:, i, :],
+                        op0=ALU.mult,
+                        op1=ALU.add,
+                        accum_out=row_sum[:, i : i + 1],
+                    )
+                    res.append(r)
+                neg_mean = stat.tile([P, UNIT_TILES], F32, tag="neg_mean")
+                nc.vector.tensor_scalar_mul(out=neg_mean[:], in0=row_sum[:], scalar1=-1.0 / D)
+
+                sq_sum = stat.tile([P, UNIT_TILES], F32, tag="sq_sum")
+                centred = []
+                for i in range(UNIT_TILES):
+                    squares = norm.tile([P, D], BF16, tag="squares", bufs=4)
+                    nc.scalar.activation(
+                        out=squares[:],
+                        in_=res[i][:],
+                        func=ACT.Square,
+                        bias=neg_mean[:, i : i + 1],
+                        scale=1.0,
+                        accum_out=sq_sum[:, i : i + 1],
+                    )
+                    cg = norm.tile([P, D], F32, tag="cg")
+                    nc.vector.scalar_tensor_tensor(
+                        out=cg[:],
+                        in0=res[i][:],
+                        scalar=neg_mean[:, i : i + 1],
+                        in1=gain[:, n, :],
+                        op0=ALU.add,
+                        op1=ALU.mult,
+                    )
+                    centred.append(cg)
+                var_eps = stat.tile([P, UNIT_TILES], F32, tag="var_eps")
+                nc.gpsimd.tensor_scalar(
+                    out=var_eps[:], in0=sq_sum[:], scalar1=1.0 / D, scalar2=EPS, op0=ALU.mult, op1=ALU.add
+                )
+                rstd = stat.tile([P, UNIT_TILES], F32, tag="rstd")
+                nc.gpsimd.tensor_tensor(out=rstd[:], in0=var_eps[:], in1=neg_half[:], op=ALU.pow)
+
+                for i in range(UNIT_TILES):
+                    yv = centred[i]
+                    nc.vector.scalar_tensor_tensor(
+                        out=yv[:],
+                        in0=yv[:],
+                        scalar=rstd[:, i : i + 1],
+                        in1=shift[:, n, :],
+                        op0=ALU.mult,
+                        op1=ALU.add,
+                    )
+                    total = acc[:, unit * UNIT_TILES + i, :]
+                    if n == 0:
+                        nc.gpsimd.tensor_tensor(out=total, in0=yv[:], in1=sel_u[:, i, :], op=ALU.mult)
+                    else:
+                        nc.gpsimd.tensor_tensor(out=yv[:], in0=yv[:], in1=sel_u[:, i, :], op=ALU.mult)
+                        nc.gpsimd.tensor_tensor(out=total, in0=total, in1=yv[:], op=ALU.add)
+                    if n == VARS - 1:
+                        first = unit * UNIT_ROWS + i * P
+                        nc.sync.dma_start(out=out[first : first + P, :], in_=total)

@@ -20,6 +20,7 @@ CHUNKS = D // P
 UNIT_ROWS = 512
 UNIT_TILES = UNIT_ROWS // P
 UNITS = BATCH // UNIT_ROWS
+TOTAL = VARS * UNITS
 EPS = 1e-5
 
 FLOPS = 3 * VARS * 2 * BATCH * D * D
@@ -30,15 +31,16 @@ def tile_variableselectionnetwork_pb_t_kernel(
 ):
     nc = tc.nc
     with ExitStack() as ctx:
+        ctx.enter_context(tc.manual_schedule())
         const = ctx.enter_context(tc.tile_pool(name="const", bufs=1))
         wstage = ctx.enter_context(tc.tile_pool(name="wstage", bufs=2))
         wquant = ctx.enter_context(tc.tile_pool(name="wquant", bufs=2))
-        loads = ctx.enter_context(tc.tile_pool(name="loads", bufs=3))
+        loads = ctx.enter_context(tc.tile_pool(name="loads", bufs=4))
         quant = ctx.enter_context(tc.tile_pool(name="quant", bufs=2))
         gate = ctx.enter_context(tc.tile_pool(name="gate", bufs=2))
-        norm = ctx.enter_context(tc.tile_pool(name="norm", bufs=8))
+        norm = ctx.enter_context(tc.tile_pool(name="norm", bufs=2 * UNIT_TILES))
         stat = ctx.enter_context(tc.tile_pool(name="stat", bufs=3))
-        psum = ctx.enter_context(tc.psum_pool(name="psum", bufs=1))
+        psum = ctx.enter_context(tc.psum_pool(name="psum", bufs=5))
 
         ident_f = const.tile([P, P], F32)
         make_identity(nc, ident_f[:])
@@ -54,10 +56,10 @@ def tile_variableselectionnetwork_pb_t_kernel(
                 out=bias_rows[k * VARS * CHUNKS : (k + 1) * VARS * CHUNKS, :],
                 in_=vec.rearrange("n (c m) -> (n c) m", m=P),
             )
-        bias_ps = psum.tile([P, P], BF16, tag="hv_t")
+        bias_ps = psum.tile([P, P], BF16, tag="to_scalar")
         nc.tensor.transpose(bias_ps[:], bias_rows[:], ident_b[:])
         bias_cols = const.tile([P, 3, VARS, CHUNKS], F32)
-        nc.vector.tensor_copy(
+        nc.scalar.copy(
             out=bias_cols[:].rearrange("p k n c -> p (k n c)"), in_=bias_ps[:, 0 : 3 * VARS * CHUNKS]
         )
 
@@ -66,33 +68,242 @@ def tile_variableselectionnetwork_pb_t_kernel(
 
         acc = const.tile([P, BATCH // P, D], F32)
 
-        def quantise_weight(dram_view, raw_view_pattern, tag):
+        tiles = {}
+
+        def live(k):
+            return 0 <= k < TOTAL
+
+        def weight_load(m):
+            n = m // 3
             raw = wstage.tile([P, PACK, D], BF16, tag="w_raw", bufs=3)
-            if raw_view_pattern is None:
-                nc.sync.dma_start(out=raw[:], in_=dram_view)
+            if m % 3 == 0:
+                nc.sync.dma_start(
+                    out=raw[:].rearrange("p (u e) c -> p u e c", u=2),
+                    in_=vW1[n].rearrange("(u p e) c -> p u e c", u=2, e=2),
+                )
             else:
-                nc.sync.dma_start(out=raw[:].rearrange(raw_view_pattern, u=2), in_=dram_view)
+                w = vW4 if m % 3 == 1 else vW5
+                nc.sync.dma_start(out=raw[:], in_=w[n].rearrange("(t p) c -> p t c", p=P))
+            tiles["w_raw", m] = raw
+
+        def weight_regroup(m):
+            raw = tiles["w_raw", m]
             grouped = wstage.tile([P, D, PACK], BF16, tag="w_grp", align_bytes=64)
-            nc.scalar.copy(
-                out=grouped[:].rearrange("p (c i) t -> p c t i", i=4),
-                in_=raw[:].rearrange("p t (c i) -> p c t i", i=4),
-            )
-            codes = wquant.tile([P, D], U32, tag=tag + "_codes", align_bytes=64)
-            scales = wquant.tile([P, D], U8, tag=tag + "_scales", align_bytes=64)
+            dst = grouped[:].rearrange("p (c i) t -> p c t i", i=4)
+            src = raw[:].rearrange("p t (c i) -> p c t i", i=4)
+            if m < 3:
+                nc.vector.tensor_copy(out=dst, in_=src)
+            else:
+                nc.scalar.copy(out=dst, in_=src)
+            tiles["w_grp", m] = grouped
+
+        def weight_quantise(m):
+            codes = wquant.tile([P, D], U32, tag="w_codes%d" % (m % 3), align_bytes=64)
+            scales = wquant.tile([P, D], U8, tag="w_scales%d" % (m % 3), align_bytes=64)
             nc.vector.quantize_mx(
                 out=codes[:].bitcast(FP8X4),
                 scales=scales[:],
-                in_=grouped[:].rearrange("p c t -> p (c t)"),
+                in_=tiles["w_grp", m][:].rearrange("p c t -> p (c t)"),
             )
-            return codes, scales
+            tiles["w_codes", m] = codes
+            tiles["w_scales", m] = scales
 
-        for n in range(VARS):
-            w1_codes, w1_scales = quantise_weight(
-                vW1[n].rearrange("(u p e) c -> p u e c", u=2, e=2), "p (u e) c -> p u e c", "w1"
+        def mx_pass(out_ps, m, c, codes, scales):
+            feats = slice(c * P, (c + 1) * P)
+            nc.tensor.matmul_mx(
+                out=out_ps,
+                lhsT=tiles["w_codes", m][:, feats].bitcast(FP8X4),
+                lhsT_scale=tiles["w_scales", m][:, feats],
+                rhs=codes[:].bitcast(FP8X4),
+                rhs_scale=scales[:],
+                start=True,
+                stop=True,
             )
-            w4_codes, w4_scales = quantise_weight(vW4[n].rearrange("(t p) c -> p t c", p=P), None, "w4")
-            w5_codes, w5_scales = quantise_weight(vW5[n].rearrange("(t p) c -> p t c", p=P), None, "w5")
-            if n == 0:
+
+        def unit_rows(dram, k):
+            first = (k % UNITS) * UNIT_ROWS
+            return dram[first : first + UNIT_ROWS, k // UNITS, :].rearrange("(i p) d -> p i d", p=P)
+
+        def load_hv(k):
+            hv_u = loads.tile([P, UNIT_TILES * D], BF16, tag="hv_u")
+            nc.sync.dma_start(out=hv_u[:].rearrange("p (i d) -> p i d", i=UNIT_TILES), in_=unit_rows(hv, k))
+            tiles["hv_u", k] = hv_u
+
+        def load_x_sel(k):
+            x_u = loads.tile([P, UNIT_TILES, D], BF16, tag="x_u")
+            nc.sync.dma_start(out=x_u[:], in_=unit_rows(x, k))
+            sel_u = loads.tile([P, UNIT_TILES, D], BF16, tag="sel_u")
+            nc.sync.dma_start(out=sel_u[:], in_=unit_rows(sel_w, k))
+            tiles["x_u", k] = x_u
+            tiles["sel_u", k] = sel_u
+
+        def hv_transpose(k):
+            hv_words = tiles["hv_u", k][:].bitcast(F32)
+            hv_grp = quant.tile([P, UNIT_ROWS * PACK], BF16, tag="hv_grp", align_bytes=64)
+            hv_grp_words = hv_grp[:].bitcast(F32).rearrange("p (b u) -> p b u", u=2)
+            for half in range(2):
+                hv_t = psum.tile([P, 2, 2 * P], F32, tag="to_scalar")
+                for u in range(2):
+                    for j in range(2):
+                        i = 2 * half + j
+                        nc.tensor.transpose(
+                            hv_t[:, u, j * P : (j + 1) * P],
+                            hv_words[:, i * 2 * P + u * P : i * 2 * P + (u + 1) * P],
+                            ident_f[:],
+                        )
+                nc.scalar.copy(
+                    out=hv_grp_words[:, half * 2 * P : (half + 1) * 2 * P, :],
+                    in_=hv_t[:].rearrange("p u b -> p b u"),
+                )
+            tiles["hv_grp", k] = hv_grp
+
+        def hv_quantise(k):
+            codes = quant.tile([P, UNIT_ROWS], U32, tag="hv_codes", align_bytes=64)
+            scales = quant.tile([P, UNIT_ROWS], U8, tag="hv_scales", align_bytes=64)
+            nc.vector.quantize_mx(out=codes[:].bitcast(FP8X4), scales=scales[:], in_=tiles["hv_grp", k][:])
+            tiles["hv_codes", k] = codes
+            tiles["hv_scales", k] = scales
+
+        def first_layer(k):
+            n = k // UNITS
+            planes = quant.tile([P, CHUNKS, UNIT_ROWS], BF16, tag="e1_planes")
+            for c in range(CHUNKS):
+                e1_ps = psum.tile([P, UNIT_ROWS], F32, tag="to_scalar")
+                mx_pass(e1_ps[:], 3 * n, c, tiles["hv_codes", k], tiles["hv_scales", k])
+                nc.scalar.activation(
+                    out=planes[:, c, :], in_=e1_ps[:], func=ACT.Identity, bias=bias_cols[:, 0, n, c : c + 1], scale=1.0
+                )
+            tiles["e1_planes", k] = planes
+
+        def e1_regroup(k):
+            grouped = quant.tile([P, UNIT_ROWS, PACK], BF16, tag="e1_grp", align_bytes=64)
+            nc.vector.tensor_copy(
+                out=grouped[:].rearrange("p (b i) t -> p b t i", i=4),
+                in_=tiles["e1_planes", k][:].rearrange("p t (b i) -> p b t i", i=4),
+            )
+            tiles["e1_grp", k] = grouped
+
+        def e1_quantise(k):
+            codes = quant.tile([P, UNIT_ROWS], U32, tag="e1_codes", align_bytes=64)
+            scales = quant.tile([P, UNIT_ROWS], U8, tag="e1_scales", align_bytes=64)
+            nc.vector.quantize_mx(
+                out=codes[:].bitcast(FP8X4),
+                scales=scales[:],
+                in_=tiles["e1_grp", k][:].rearrange("p b t -> p (b t)"),
+            )
+            tiles["e1_codes", k] = codes
+            tiles["e1_scales", k] = scales
+
+        def gate_layers(k):
+            n = k // UNITS
+            gv_t = gate.tile([P, CHUNKS, UNIT_ROWS], F32, tag="gv_t")
+            for c in range(CHUNKS):
+                g4_ps = psum.tile([P, UNIT_ROWS], F32, tag="to_scalar")
+                mx_pass(g4_ps[:], 3 * n + 1, c, tiles["e1_codes", k], tiles["e1_scales", k])
+                g5_ps = psum.tile([P, UNIT_ROWS], F32, tag="to_vector", bufs=3)
+                mx_pass(g5_ps[:], 3 * n + 2, c, tiles["e1_codes", k], tiles["e1_scales", k])
+                sig = gate.tile([P, UNIT_ROWS], F32, tag="sig", bufs=3)
+                nc.scalar.activation(
+                    out=sig[:], in_=g4_ps[:], func=ACT.Sigmoid, bias=bias_cols[:, 1, n, c : c + 1], scale=1.0
+                )
+                nc.vector.scalar_tensor_tensor(
+                    out=gv_t[:, c, :],
+                    in0=g5_ps[:],
+                    scalar=bias_cols[:, 2, n, c : c + 1],
+                    in1=sig[:],
+                    op0=ALU.add,
+                    op1=ALU.mult,
+                )
+            tiles["gv_t", k] = gv_t
+
+        def residual(k):
+            row_sum = stat.tile([P, UNIT_TILES], F32, tag="row_sum")
+            for i in range(UNIT_TILES):
+                r_ps = psum.tile([P, D], F32, tag="to_scalar")
+                nc.tensor.matmul(out=r_ps[:], lhsT=ident_b[:], rhs=tiles["x_u", k][:, i, :], start=True, stop=False)
+                for c in range(CHUNKS):
+                    nc.tensor.matmul(
+                        out=r_ps[:, c * P : (c + 1) * P],
+                        lhsT=tiles["gv_t", k][:, c, i * P : (i + 1) * P],
+                        rhs=ident_f[:],
+                        is_transpose=True,
+                        start=False,
+                        stop=(c == CHUNKS - 1),
+                    )
+                r = norm.tile([P, D], F32, tag="r")
+                nc.scalar.activation(out=r[:], in_=r_ps[:], func=ACT.Identity, accum_out=row_sum[:, i : i + 1])
+                tiles["r%d" % i, k] = r
+            tiles["row_sum", k] = row_sum
+
+        def mean(k):
+            neg_mean = stat.tile([P, UNIT_TILES], F32, tag="neg_mean")
+            nc.scalar.mul(out=neg_mean[:], in_=tiles["row_sum", k][:], mul=-1.0 / D)
+            tiles["neg_mean", k] = neg_mean
+
+        def centre(k):
+            n = k // UNITS
+            neg_mean = tiles["neg_mean", k]
+            sq_sum = stat.tile([P, UNIT_TILES], F32, tag="sq_sum")
+            yv = gate.tile([P, UNIT_TILES, D], F32, tag="yv")
+            for i in range(UNIT_TILES):
+                r = tiles["r%d" % i, k]
+                squares = norm.tile([P, D], BF16, tag="squares", bufs=4)
+                nc.scalar.activation(
+                    out=squares[:],
+                    in_=r[:],
+                    func=ACT.Square,
+                    bias=neg_mean[:, i : i + 1],
+                    scale=1.0,
+                    accum_out=sq_sum[:, i : i + 1],
+                )
+                nc.vector.scalar_tensor_tensor(
+                    out=yv[:, i, :], in0=r[:], scalar=neg_mean[:, i : i + 1], in1=gain[:, n, :], op0=ALU.add, op1=ALU.mult
+                )
+            tiles["yv", k] = yv
+            var_eps = stat.tile([P, UNIT_TILES], F32, tag="var_eps")
+            nc.scalar.activation(out=var_eps[:], in_=sq_sum[:], func=ACT.Copy, bias=EPS, scale=1.0 / D)
+            rstd = stat.tile([P, UNIT_TILES], F32, tag="rstd")
+            nc.gpsimd.tensor_tensor(out=rstd[:], in0=var_eps[:], in1=neg_half[:], op=ALU.pow)
+            tiles["rstd", k] = rstd
+
+        def unit_acc(k):
+            first = (k % UNITS) * UNIT_TILES
+            return acc[:, first : first + UNIT_TILES, :]
+
+        def scale_shift(k):
+            n = k // UNITS
+            yv = tiles["yv", k]
+            for i in range(UNIT_TILES):
+                nc.vector.scalar_tensor_tensor(
+                    out=yv[:, i, :],
+                    in0=yv[:, i, :],
+                    scalar=tiles["rstd", k][:, i : i + 1],
+                    in1=shift[:, n, :],
+                    op0=ALU.mult,
+                    op1=ALU.add,
+                )
+
+        def weigh(k):
+            yv = tiles["yv", k]
+            dst = unit_acc(k) if k // UNITS == 0 else yv[:]
+            nc.vector.tensor_tensor(out=dst, in0=yv[:], in1=tiles["sel_u", k][:], op=ALU.mult)
+
+        def accumulate(k):
+            for i in range(UNIT_TILES):
+                tile_no = (k % UNITS) * UNIT_TILES + i
+                if k // UNITS > 0:
+                    nc.vector.tensor_tensor(
+                        out=acc[:, tile_no, :], in0=acc[:, tile_no, :], in1=tiles["yv", k][:, i, :], op=ALU.add
+                    )
+                if k // UNITS == VARS - 1:
+                    nc.sync.dma_start(out=out[tile_no * P : (tile_no + 1) * P, :], in_=acc[:, tile_no, :])
+
+        for step in range(-5, TOTAL + 1):
+            if live(step + 4):
+                load_hv(step + 4)
+            if live(step + 5):
+                weight_load(step + 5)
+            if step == -2:
                 nc.sync.dma_start(
                     out=gain[:].rearrange("p n d -> p (n d)"),
                     in_=vlng.rearrange("n d -> (n d)").partition_broadcast(P),
@@ -101,171 +312,34 @@ def tile_variableselectionnetwork_pb_t_kernel(
                     out=shift[:].rearrange("p n d -> p (n d)"),
                     in_=vlnb.rearrange("n d -> (n d)").partition_broadcast(P),
                 )
+            if live(step + 1):
+                load_x_sel(step + 1)
 
-            for unit in range(UNITS):
-                rows = slice(unit * UNIT_ROWS, (unit + 1) * UNIT_ROWS)
-                hv_u = loads.tile([P, UNIT_TILES * D], BF16, tag="hv_u")
-                nc.sync.dma_start(
-                    out=hv_u[:].rearrange("p (i d) -> p i d", i=UNIT_TILES),
-                    in_=hv[rows, n, :].rearrange("(i p) d -> p i d", p=P),
-                )
-                x_u = loads.tile([P, UNIT_TILES, D], BF16, tag="x_u")
-                nc.sync.dma_start(out=x_u[:], in_=x[rows, n, :].rearrange("(i p) d -> p i d", p=P))
-                sel_u = loads.tile([P, UNIT_TILES, D], BF16, tag="sel_u")
-                nc.sync.dma_start(out=sel_u[:], in_=sel_w[rows, n, :].rearrange("(i p) d -> p i d", p=P))
-
-                hv_words = hv_u[:].bitcast(F32)
-                hv_grp = quant.tile([P, UNIT_ROWS * PACK], BF16, tag="hv_grp", align_bytes=64)
-                hv_grp_words = hv_grp[:].bitcast(F32).rearrange("p (b u) -> p b u", u=2)
-                for half in range(2):
-                    hv_t = psum.tile([P, 2, 2 * P], F32, tag="hv_t")
-                    for u in range(2):
-                        for k in range(2):
-                            i = 2 * half + k
-                            nc.tensor.transpose(
-                                hv_t[:, u, k * P : (k + 1) * P],
-                                hv_words[:, i * 2 * P + u * P : i * 2 * P + (u + 1) * P],
-                                ident_f[:],
-                            )
-                    nc.scalar.copy(
-                        out=hv_grp_words[:, half * 2 * P : (half + 1) * 2 * P, :],
-                        in_=hv_t[:].rearrange("p u b -> p b u"),
-                    )
-                hv_codes = quant.tile([P, UNIT_ROWS], U32, tag="hv_codes", align_bytes=64)
-                hv_scales = quant.tile([P, UNIT_ROWS], U8, tag="hv_scales", align_bytes=64)
-                nc.vector.quantize_mx(out=hv_codes[:].bitcast(FP8X4), scales=hv_scales[:], in_=hv_grp[:])
-
-                e1_grp = quant.tile([P, UNIT_ROWS, PACK], BF16, tag="e1_grp", align_bytes=64)
-                for i in range(UNIT_TILES):
-                    cols = slice(i * P, (i + 1) * P)
-                    e1_ps = psum.tile([P, CHUNKS, P], F32, tag="e1_ps", bufs=2)
-                    for c in range(CHUNKS):
-                        nc.tensor.matmul_mx(
-                            out=e1_ps[:, c, :],
-                            lhsT=w1_codes[:, c * P : (c + 1) * P].bitcast(FP8X4),
-                            lhsT_scale=w1_scales[:, c * P : (c + 1) * P],
-                            rhs=hv_codes[:, cols].bitcast(FP8X4),
-                            rhs_scale=hv_scales[:, cols],
-                            start=True,
-                            stop=True,
-                        )
-                    nc.vector.tensor_tensor(
-                        out=e1_grp[:, cols, :],
-                        in0=e1_ps[:].rearrange("p c b -> p b c"),
-                        in1=bias_cols[:, 0, n, :].unsqueeze(1).to_broadcast([P, P, CHUNKS]),
-                        op=ALU.add,
-                    )
-                e1_codes = quant.tile([P, UNIT_ROWS], U32, tag="e1_codes", align_bytes=64)
-                e1_scales = quant.tile([P, UNIT_ROWS], U8, tag="e1_scales", align_bytes=64)
-                nc.vector.quantize_mx(
-                    out=e1_codes[:].bitcast(FP8X4),
-                    scales=e1_scales[:],
-                    in_=e1_grp[:].rearrange("p b t -> p (b t)"),
-                )
-
-                gv_t = gate.tile([P, CHUNKS, UNIT_ROWS], F32, tag="gv_t")
-                for c in range(CHUNKS):
-                    feats = slice(c * P, (c + 1) * P)
-                    g4_ps = psum.tile([P, UNIT_ROWS], F32, tag="g4_ps")
-                    nc.tensor.matmul_mx(
-                        out=g4_ps[:],
-                        lhsT=w4_codes[:, feats].bitcast(FP8X4),
-                        lhsT_scale=w4_scales[:, feats],
-                        rhs=e1_codes[:].bitcast(FP8X4),
-                        rhs_scale=e1_scales[:],
-                        start=True,
-                        stop=True,
-                    )
-                    g5_ps = psum.tile([P, UNIT_ROWS], F32, tag="g5_ps", bufs=2)
-                    nc.tensor.matmul_mx(
-                        out=g5_ps[:],
-                        lhsT=w5_codes[:, feats].bitcast(FP8X4),
-                        lhsT_scale=w5_scales[:, feats],
-                        rhs=e1_codes[:].bitcast(FP8X4),
-                        rhs_scale=e1_scales[:],
-                        start=True,
-                        stop=True,
-                    )
-                    sig = gate.tile([P, UNIT_ROWS], F32, tag="sig", bufs=3)
-                    nc.scalar.activation(
-                        out=sig[:], in_=g4_ps[:], func=ACT.Sigmoid, bias=bias_cols[:, 1, n, c : c + 1], scale=1.0
-                    )
-                    nc.vector.scalar_tensor_tensor(
-                        out=gv_t[:, c, :],
-                        in0=g5_ps[:],
-                        scalar=bias_cols[:, 2, n, c : c + 1],
-                        in1=sig[:],
-                        op0=ALU.add,
-                        op1=ALU.mult,
-                    )
-
-                row_sum = stat.tile([P, UNIT_TILES], F32, tag="row_sum")
-                res = []
-                for i in range(UNIT_TILES):
-                    gv_ps = psum.tile([P, D], F32, tag="gv_ps", bufs=2)
-                    for c in range(CHUNKS):
-                        nc.tensor.transpose(
-                            gv_ps[:, c * P : (c + 1) * P], gv_t[:, c, i * P : (i + 1) * P], ident_f[:]
-                        )
-                    r = norm.tile([P, D], F32, tag="r")
-                    nc.vector.scalar_tensor_tensor(
-                        out=r[:],
-                        in0=gv_ps[:],
-                        scalar=1.0,
-                        in1=x_u[:, i, :],
-                        op0=ALU.mult,
-                        op1=ALU.add,
-                        accum_out=row_sum[:, i : i + 1],
-                    )
-                    res.append(r)
-                neg_mean = stat.tile([P, UNIT_TILES], F32, tag="neg_mean")
-                nc.vector.tensor_scalar_mul(out=neg_mean[:], in0=row_sum[:], scalar1=-1.0 / D)
-
-                sq_sum = stat.tile([P, UNIT_TILES], F32, tag="sq_sum")
-                centred = []
-                for i in range(UNIT_TILES):
-                    squares = norm.tile([P, D], BF16, tag="squares", bufs=4)
-                    nc.scalar.activation(
-                        out=squares[:],
-                        in_=res[i][:],
-                        func=ACT.Square,
-                        bias=neg_mean[:, i : i + 1],
-                        scale=1.0,
-                        accum_out=sq_sum[:, i : i + 1],
-                    )
-                    cg = norm.tile([P, D], F32, tag="cg")
-                    nc.vector.scalar_tensor_tensor(
-                        out=cg[:],
-                        in0=res[i][:],
-                        scalar=neg_mean[:, i : i + 1],
-                        in1=gain[:, n, :],
-                        op0=ALU.add,
-                        op1=ALU.mult,
-                    )
-                    centred.append(cg)
-                var_eps = stat.tile([P, UNIT_TILES], F32, tag="var_eps")
-                nc.gpsimd.tensor_scalar(
-                    out=var_eps[:], in0=sq_sum[:], scalar1=1.0 / D, scalar2=EPS, op0=ALU.mult, op1=ALU.add
-                )
-                rstd = stat.tile([P, UNIT_TILES], F32, tag="rstd")
-                nc.gpsimd.tensor_tensor(out=rstd[:], in0=var_eps[:], in1=neg_half[:], op=ALU.pow)
-
-                for i in range(UNIT_TILES):
-                    yv = centred[i]
-                    nc.vector.scalar_tensor_tensor(
-                        out=yv[:],
-                        in0=yv[:],
-                        scalar=rstd[:, i : i + 1],
-                        in1=shift[:, n, :],
-                        op0=ALU.mult,
-                        op1=ALU.add,
-                    )
-                    total = acc[:, unit * UNIT_TILES + i, :]
-                    if n == 0:
-                        nc.gpsimd.tensor_tensor(out=total, in0=yv[:], in1=sel_u[:, i, :], op=ALU.mult)
-                    else:
-                        nc.gpsimd.tensor_tensor(out=yv[:], in0=yv[:], in1=sel_u[:, i, :], op=ALU.mult)
-                        nc.gpsimd.tensor_tensor(out=total, in0=total, in1=yv[:], op=ALU.add)
-                    if n == VARS - 1:
-                        first = unit * UNIT_ROWS + i * P
-                        nc.sync.dma_start(out=out[first : first + P, :], in_=total)
+            if live(step):
+                gate_layers(step)
+            if live(step + 1):
+                first_layer(step + 1)
+            if live(step):
+                residual(step)
+            if live(step):
+                mean(step)
+            if live(step - 1):
+                scale_shift(step - 1)
+            if live(step + 1):
+                e1_regroup(step + 1)
+            if live(step - 1):
+                weigh(step - 1)
+            if live(step + 1):
+                e1_quantise(step + 1)
+            if live(step - 1):
+                accumulate(step - 1)
+            if live(step):
+                centre(step)
+            if live(step + 2):
+                hv_transpose(step + 2)
+            if live(step + 2):
+                hv_quantise(step + 2)
+            if live(step + 3):
+                weight_quantise(step + 3)
+            if live(step + 4):
+                weight_regroup(step + 4)

@@ -40,7 +40,7 @@ def tile_variableselectionnetwork_pb_t_kernel(
         gate = ctx.enter_context(tc.tile_pool(name="gate", bufs=2))
         norm = ctx.enter_context(tc.tile_pool(name="norm", bufs=2 * UNIT_TILES))
         stat = ctx.enter_context(tc.tile_pool(name="stat", bufs=3))
-        psum = ctx.enter_context(tc.psum_pool(name="psum", bufs=5))
+        psum = ctx.enter_context(tc.psum_pool(name="psum", bufs=4))
 
         ident_f = const.tile([P, P], F32)
         make_identity(nc, ident_f[:])
@@ -240,6 +240,12 @@ def tile_variableselectionnetwork_pb_t_kernel(
             nc.scalar.mul(out=neg_mean[:], in_=tiles["row_sum", k][:], mul=-1.0 / D)
             tiles["neg_mean", k] = neg_mean
 
+        def spread_gain_shift(n):
+            gs_ps = psum.tile([P, 2, D], BF16, tag="gain_shift", bufs=1)
+            nc.tensor.matmul(out=gs_ps[:, 0, :], lhsT=ident_b[:], rhs=gain[:, n, :], start=True, stop=True)
+            nc.tensor.matmul(out=gs_ps[:, 1, :], lhsT=ident_b[:], rhs=shift[:, n, :], start=True, stop=True)
+            tiles["gain_shift", n] = gs_ps
+
         def centre(k):
             n = k // UNITS
             neg_mean = tiles["neg_mean", k]
@@ -257,7 +263,8 @@ def tile_variableselectionnetwork_pb_t_kernel(
                     accum_out=sq_sum[:, i : i + 1],
                 )
                 nc.vector.scalar_tensor_tensor(
-                    out=yv[:, i, :], in0=r[:], scalar=neg_mean[:, i : i + 1], in1=gain[:, n, :], op0=ALU.add, op1=ALU.mult
+                    out=yv[:, i, :], in0=r[:], scalar=neg_mean[:, i : i + 1], in1=tiles["gain_shift", n][:, 0, :],
+                    op0=ALU.add, op1=ALU.mult,
                 )
             tiles["yv", k] = yv
             var_eps = stat.tile([P, UNIT_TILES], F32, tag="var_eps")
@@ -278,7 +285,7 @@ def tile_variableselectionnetwork_pb_t_kernel(
                     out=yv[:, i, :],
                     in0=yv[:, i, :],
                     scalar=tiles["rstd", k][:, i : i + 1],
-                    in1=shift[:, n, :],
+                    in1=tiles["gain_shift", n][:, 1, :],
                     op0=ALU.mult,
                     op1=ALU.add,
                 )
@@ -288,11 +295,12 @@ def tile_variableselectionnetwork_pb_t_kernel(
             dst = unit_acc(k) if k // UNITS == 0 else yv[:]
             nc.vector.tensor_tensor(out=dst, in0=yv[:], in1=tiles["sel_u", k][:], op=ALU.mult)
 
-        def accumulate(k):
-            for i in range(UNIT_TILES):
+        def accumulate(k, first_tile):
+            adder = nc.vector if k == TOTAL - 1 else nc.gpsimd
+            for i in range(first_tile, first_tile + UNIT_TILES // 2):
                 tile_no = (k % UNITS) * UNIT_TILES + i
                 if k // UNITS > 0:
-                    nc.vector.tensor_tensor(
+                    adder.tensor_tensor(
                         out=acc[:, tile_no, :], in0=acc[:, tile_no, :], in1=tiles["yv", k][:, i, :], op=ALU.add
                     )
                 if k // UNITS == VARS - 1:
@@ -321,10 +329,11 @@ def tile_variableselectionnetwork_pb_t_kernel(
                 first_layer(step + 1)
             if live(step):
                 residual(step)
-            if live(step):
                 mean(step)
             if live(step - 1):
                 scale_shift(step - 1)
+            if live(step) and step % UNITS == 0:
+                spread_gain_shift(step // UNITS)
             if live(step + 1):
                 e1_regroup(step + 1)
             if live(step - 1):
@@ -332,12 +341,13 @@ def tile_variableselectionnetwork_pb_t_kernel(
             if live(step + 1):
                 e1_quantise(step + 1)
             if live(step - 1):
-                accumulate(step - 1)
+                accumulate(step - 1, 0)
             if live(step):
                 centre(step)
+            if live(step - 1):
+                accumulate(step - 1, UNIT_TILES // 2)
             if live(step + 2):
                 hv_transpose(step + 2)
-            if live(step + 2):
                 hv_quantise(step + 2)
             if live(step + 3):
                 weight_quantise(step + 3)

@@ -34,7 +34,7 @@ def tile_variableselectionnetwork_pb_t_kernel(
         ctx.enter_context(tc.manual_schedule())
         const = ctx.enter_context(tc.tile_pool(name="const", bufs=1))
         wstage = ctx.enter_context(tc.tile_pool(name="wstage", bufs=2))
-        wquant = ctx.enter_context(tc.tile_pool(name="wquant", bufs=2))
+        wquant = ctx.enter_context(tc.tile_pool(name="wquant", bufs=VARS))
         loads = ctx.enter_context(tc.tile_pool(name="loads", bufs=4))
         quant = ctx.enter_context(tc.tile_pool(name="quant", bufs=2))
         gate = ctx.enter_context(tc.tile_pool(name="gate", bufs=2))
@@ -52,10 +52,15 @@ def tile_variableselectionnetwork_pb_t_kernel(
         bias_rows = const.tile([P, P], BF16)
         nc.vector.memset(bias_rows[:], 0.0)
         for k, vec in enumerate((vb1, vb4, vb5)):
-            nc.sync.dma_start(
+            nc.scalar.dma_start(
                 out=bias_rows[k * VARS * CHUNKS : (k + 1) * VARS * CHUNKS, :],
                 in_=vec.rearrange("n (c m) -> (n c) m", m=P),
             )
+        gs_rows = const.tile([P, D], BF16)
+        nc.vector.memset(gs_rows[:], 0.0)
+        nc.scalar.dma_start(out=gs_rows[0:VARS, :], in_=vlng)
+        nc.scalar.dma_start(out=gs_rows[VARS : 2 * VARS, :], in_=vlnb)
+
         bias_ps = psum.tile([P, P], BF16, tag="to_scalar")
         nc.tensor.transpose(bias_ps[:], bias_rows[:], ident_b[:])
         bias_cols = const.tile([P, 3, VARS, CHUNKS], F32)
@@ -63,8 +68,6 @@ def tile_variableselectionnetwork_pb_t_kernel(
             out=bias_cols[:].rearrange("p k n c -> p (k n c)"), in_=bias_ps[:, 0 : 3 * VARS * CHUNKS]
         )
 
-        gain = const.tile([P, VARS, D], BF16)
-        shift = const.tile([P, VARS, D], BF16)
 
         acc = const.tile([P, BATCH // P, D], F32)
 
@@ -75,7 +78,7 @@ def tile_variableselectionnetwork_pb_t_kernel(
 
         def weight_load(m):
             n = m // 3
-            raw = wstage.tile([P, PACK, D], BF16, tag="w_raw", bufs=3)
+            raw = wstage.tile([P, PACK, D], BF16, tag="w_raw", bufs=4)
             if m % 3 == 0:
                 nc.sync.dma_start(
                     out=raw[:].rearrange("p (u e) c -> p u e c", u=2),
@@ -89,12 +92,14 @@ def tile_variableselectionnetwork_pb_t_kernel(
         def weight_regroup(m):
             raw = tiles["w_raw", m]
             grouped = wstage.tile([P, D, PACK], BF16, tag="w_grp", align_bytes=64)
-            dst = grouped[:].rearrange("p (c i) t -> p c t i", i=4)
-            src = raw[:].rearrange("p t (c i) -> p c t i", i=4)
-            if m < 3:
-                nc.vector.tensor_copy(out=dst, in_=src)
-            else:
-                nc.scalar.copy(out=dst, in_=src)
+            nc.vector.tensor_copy(
+                out=grouped[:, 0:256, :].rearrange("p (c i) t -> p c t i", i=4),
+                in_=raw[:, :, 0:256].rearrange("p t (c i) -> p c t i", i=4),
+            )
+            nc.scalar.copy(
+                out=grouped[:, 256:D, :].rearrange("p (c i) t -> p c t i", i=4),
+                in_=raw[:, :, 256:D].rearrange("p t (c i) -> p c t i", i=4),
+            )
             tiles["w_grp", m] = grouped
 
         def weight_quantise(m):
@@ -130,7 +135,7 @@ def tile_variableselectionnetwork_pb_t_kernel(
             tiles["hv_u", k] = hv_u
 
         def load_x_sel(k):
-            x_u = loads.tile([P, UNIT_TILES, D], BF16, tag="x_u")
+            x_u = loads.tile([P, UNIT_TILES, D], BF16, tag="x_u", bufs=3)
             nc.sync.dma_start(out=x_u[:], in_=unit_rows(x, k))
             sel_u = loads.tile([P, UNIT_TILES, D], BF16, tag="sel_u")
             nc.sync.dma_start(out=sel_u[:], in_=unit_rows(sel_w, k))
@@ -242,8 +247,15 @@ def tile_variableselectionnetwork_pb_t_kernel(
 
         def spread_gain_shift(n):
             gs_ps = psum.tile([P, 2, D], BF16, tag="gain_shift", bufs=1)
-            nc.tensor.matmul(out=gs_ps[:, 0, :], lhsT=ident_b[:], rhs=gain[:, n, :], start=True, stop=True)
-            nc.tensor.matmul(out=gs_ps[:, 1, :], lhsT=ident_b[:], rhs=shift[:, n, :], start=True, stop=True)
+            for v in range(2):
+                row = v * VARS + n
+                nc.tensor.matmul(
+                    out=gs_ps[:, v, :],
+                    lhsT=ident_b[:, row : row + 1].to_broadcast([P, P]),
+                    rhs=gs_rows[:],
+                    start=True,
+                    stop=True,
+                )
             tiles["gain_shift", n] = gs_ps
 
         def centre(k):
@@ -306,23 +318,18 @@ def tile_variableselectionnetwork_pb_t_kernel(
                 if k // UNITS == VARS - 1:
                     nc.sync.dma_start(out=out[tile_no * P : (tile_no + 1) * P, :], in_=acc[:, tile_no, :])
 
-        for step in range(-5, TOTAL + 1):
+        for step in range(-4, TOTAL + 1):
             if live(step + 4):
                 load_hv(step + 4)
-            if live(step + 5):
-                weight_load(step + 5)
-            if step == -2:
-                nc.sync.dma_start(
-                    out=gain[:].rearrange("p n d -> p (n d)"),
-                    in_=vlng.rearrange("n d -> (n d)").partition_broadcast(P),
-                )
-                nc.sync.dma_start(
-                    out=shift[:].rearrange("p n d -> p (n d)"),
-                    in_=vlnb.rearrange("n d -> (n d)").partition_broadcast(P),
-                )
             if live(step + 1):
                 load_x_sel(step + 1)
+            for m in (2 * step + 7, 2 * step + 8):
+                if live(m):
+                    weight_load(m)
 
+            for m in (2 * step + 3, 2 * step + 4):
+                if live(m):
+                    weight_quantise(m)
             if live(step):
                 gate_layers(step)
             if live(step + 1):
@@ -349,7 +356,6 @@ def tile_variableselectionnetwork_pb_t_kernel(
             if live(step + 2):
                 hv_transpose(step + 2)
                 hv_quantise(step + 2)
-            if live(step + 3):
-                weight_quantise(step + 3)
-            if live(step + 4):
-                weight_regroup(step + 4)
+            for m in (2 * step + 5, 2 * step + 6):
+                if live(m):
+                    weight_regroup(m)

@@ -93,12 +93,12 @@ def tile_variableselectionnetwork_pb_t_kernel(
             raw = tiles["w_raw", m]
             grouped = wstage.tile([P, D, PACK], BF16, tag="w_grp", align_bytes=64)
             nc.vector.tensor_copy(
-                out=grouped[:, 0:256, :].rearrange("p (c i) t -> p c t i", i=4),
-                in_=raw[:, :, 0:256].rearrange("p t (c i) -> p c t i", i=4),
+                out=grouped[:, 0:320, :].rearrange("p (c i) t -> p c t i", i=4),
+                in_=raw[:, :, 0:320].rearrange("p t (c i) -> p c t i", i=4),
             )
             nc.scalar.copy(
-                out=grouped[:, 256:D, :].rearrange("p (c i) t -> p c t i", i=4),
-                in_=raw[:, :, 256:D].rearrange("p t (c i) -> p c t i", i=4),
+                out=grouped[:, 320:D, :].rearrange("p (c i) t -> p c t i", i=4),
+                in_=raw[:, :, 320:D].rearrange("p t (c i) -> p c t i", i=4),
             )
             tiles["w_grp", m] = grouped
 
@@ -142,11 +142,14 @@ def tile_variableselectionnetwork_pb_t_kernel(
             tiles["x_u", k] = x_u
             tiles["sel_u", k] = sel_u
 
-        def hv_transpose(k):
+        def hv_transpose(k, half):
             hv_words = tiles["hv_u", k][:].bitcast(F32)
-            hv_grp = quant.tile([P, UNIT_ROWS * PACK], BF16, tag="hv_grp", align_bytes=64)
+            if half == 0:
+                hv_grp = quant.tile([P, UNIT_ROWS * PACK], BF16, tag="hv_grp", align_bytes=64)
+            else:
+                hv_grp = tiles["hv_grp", k]
             hv_grp_words = hv_grp[:].bitcast(F32).rearrange("p (b u) -> p b u", u=2)
-            for half in range(2):
+            if True:
                 hv_t = psum.tile([P, 2, 2 * P], F32, tag="to_scalar")
                 for u in range(2):
                     for j in range(2):
@@ -304,8 +307,13 @@ def tile_variableselectionnetwork_pb_t_kernel(
 
         def weigh(k):
             yv = tiles["yv", k]
-            dst = unit_acc(k) if k // UNITS == 0 else yv[:]
-            nc.vector.tensor_tensor(out=dst, in0=yv[:], in1=tiles["sel_u", k][:], op=ALU.mult)
+            if k // UNITS == 0:
+                for i in range(UNIT_TILES):
+                    nc.gpsimd.tensor_tensor(
+                        out=unit_acc(k)[:, i, :], in0=yv[:, i, :], in1=tiles["sel_u", k][:, i, :], op=ALU.mult
+                    )
+            else:
+                nc.vector.tensor_tensor(out=yv[:], in0=yv[:], in1=tiles["sel_u", k][:], op=ALU.mult)
 
         def accumulate(k, first_tile):
             adder = nc.vector if k == TOTAL - 1 else nc.gpsimd
@@ -336,7 +344,12 @@ def tile_variableselectionnetwork_pb_t_kernel(
                 first_layer(step + 1)
             if live(step):
                 residual(step)
+            if live(step + 2):
+                hv_transpose(step + 2, 0)
+            if live(step):
                 mean(step)
+            if live(step + 2):
+                hv_transpose(step + 2, 1)
             if live(step - 1):
                 scale_shift(step - 1)
             if live(step) and step % UNITS == 0:
@@ -354,7 +367,6 @@ def tile_variableselectionnetwork_pb_t_kernel(
             if live(step - 1):
                 accumulate(step - 1, UNIT_TILES // 2)
             if live(step + 2):
-                hv_transpose(step + 2)
                 hv_quantise(step + 2)
             for m in (2 * step + 5, 2 * step + 6):
                 if live(m):

@@ -13,6 +13,7 @@ ACT = mybir.ActivationFunctionType
 
 P = 128
 PACK = 4
+PAIR = 2
 BATCH = 1536
 VARS = 4
 D = 512
@@ -21,9 +22,15 @@ UNIT_ROWS = 512
 UNIT_TILES = UNIT_ROWS // P
 UNITS = BATCH // UNIT_ROWS
 TOTAL = VARS * UNITS
+MATRICES = 3
+WEIGHTS = MATRICES * VARS
+WEIGHTS_A_STEP = 2
+LEAD = 4
+RUN = 4
+VECTOR_COLUMNS = 320
 EPS = 1e-5
 
-FLOPS = 3 * VARS * 2 * BATCH * D * D
+FLOPS = MATRICES * VARS * 2 * BATCH * D * D
 
 
 def tile_variableselectionnetwork_pb_t_kernel(
@@ -33,7 +40,7 @@ def tile_variableselectionnetwork_pb_t_kernel(
     with ExitStack() as ctx:
         ctx.enter_context(tc.manual_schedule())
         const = ctx.enter_context(tc.tile_pool(name="const", bufs=1))
-        wstage = ctx.enter_context(tc.tile_pool(name="wstage", bufs=2))
+        wstage = ctx.enter_context(tc.tile_pool(name="wstage", bufs=WEIGHTS_A_STEP))
         wquant = ctx.enter_context(tc.tile_pool(name="wquant", bufs=VARS))
         loads = ctx.enter_context(tc.tile_pool(name="loads", bufs=4))
         quant = ctx.enter_context(tc.tile_pool(name="quant", bufs=2))
@@ -48,6 +55,8 @@ def tile_variableselectionnetwork_pb_t_kernel(
         make_identity(nc, ident_b[:])
         neg_half = const.tile([P, UNIT_TILES], F32)
         nc.vector.memset(neg_half[:], -0.5)
+        warm = const.tile([P, UNIT_TILES], F32)
+        nc.scalar.activation(out=warm[:], in_=neg_half[:], func=ACT.Sigmoid)
 
         bias_rows = const.tile([P, P], BF16)
         nc.vector.memset(bias_rows[:], 0.0)
@@ -63,29 +72,25 @@ def tile_variableselectionnetwork_pb_t_kernel(
 
         bias_ps = psum.tile([P, P], BF16, tag="to_scalar")
         nc.tensor.transpose(bias_ps[:], bias_rows[:], ident_b[:])
-        bias_cols = const.tile([P, 3, VARS, CHUNKS], F32)
+        bias_cols = const.tile([P, MATRICES, VARS, CHUNKS], F32)
         nc.scalar.copy(
-            out=bias_cols[:].rearrange("p k n c -> p (k n c)"), in_=bias_ps[:, 0 : 3 * VARS * CHUNKS]
+            out=bias_cols[:].rearrange("p k n c -> p (k n c)"), in_=bias_ps[:, 0 : MATRICES * VARS * CHUNKS]
         )
-
 
         acc = const.tile([P, BATCH // P, D], F32)
 
         tiles = {}
 
-        def live(k):
-            return 0 <= k < TOTAL
-
         def weight_load(m):
-            n = m // 3
-            raw = wstage.tile([P, PACK, D], BF16, tag="w_raw", bufs=4)
-            if m % 3 == 0:
+            n = m // MATRICES
+            raw = wstage.tile([P, PACK, D], BF16, tag="w_raw", bufs=2 * WEIGHTS_A_STEP)
+            if m % MATRICES == 0:
                 nc.sync.dma_start(
-                    out=raw[:].rearrange("p (u e) c -> p u e c", u=2),
-                    in_=vW1[n].rearrange("(u p e) c -> p u e c", u=2, e=2),
+                    out=raw[:].rearrange("p (u e) c -> p u e c", e=PAIR),
+                    in_=vW1[n].rearrange("(u p e) c -> p u e c", p=P, e=PAIR),
                 )
             else:
-                w = vW4 if m % 3 == 1 else vW5
+                w = vW4 if m % MATRICES == 1 else vW5
                 nc.sync.dma_start(out=raw[:], in_=w[n].rearrange("(t p) c -> p t c", p=P))
             tiles["w_raw", m] = raw
 
@@ -93,18 +98,18 @@ def tile_variableselectionnetwork_pb_t_kernel(
             raw = tiles["w_raw", m]
             grouped = wstage.tile([P, D, PACK], BF16, tag="w_grp", align_bytes=64)
             nc.vector.tensor_copy(
-                out=grouped[:, 0:320, :].rearrange("p (c i) t -> p c t i", i=4),
-                in_=raw[:, :, 0:320].rearrange("p t (c i) -> p c t i", i=4),
+                out=grouped[:, 0:VECTOR_COLUMNS, :].rearrange("p (c i) t -> p c t i", i=RUN),
+                in_=raw[:, :, 0:VECTOR_COLUMNS].rearrange("p t (c i) -> p c t i", i=RUN),
             )
             nc.scalar.copy(
-                out=grouped[:, 320:D, :].rearrange("p (c i) t -> p c t i", i=4),
-                in_=raw[:, :, 320:D].rearrange("p t (c i) -> p c t i", i=4),
+                out=grouped[:, VECTOR_COLUMNS:D, :].rearrange("p (c i) t -> p c t i", i=RUN),
+                in_=raw[:, :, VECTOR_COLUMNS:D].rearrange("p t (c i) -> p c t i", i=RUN),
             )
             tiles["w_grp", m] = grouped
 
         def weight_quantise(m):
-            codes = wquant.tile([P, D], U32, tag="w_codes%d" % (m % 3), align_bytes=64)
-            scales = wquant.tile([P, D], U8, tag="w_scales%d" % (m % 3), align_bytes=64)
+            codes = wquant.tile([P, D], U32, tag="w_codes%d" % (m % MATRICES), align_bytes=64)
+            scales = wquant.tile([P, D], U8, tag="w_scales%d" % (m % MATRICES), align_bytes=64)
             nc.vector.quantize_mx(
                 out=codes[:].bitcast(FP8X4),
                 scales=scales[:],
@@ -113,17 +118,24 @@ def tile_variableselectionnetwork_pb_t_kernel(
             tiles["w_codes", m] = codes
             tiles["w_scales", m] = scales
 
-        def mx_pass(out_ps, m, c, codes, scales):
+        def mx_pass(out_ps, m, c, operand, k):
             feats = slice(c * P, (c + 1) * P)
             nc.tensor.matmul_mx(
                 out=out_ps,
                 lhsT=tiles["w_codes", m][:, feats].bitcast(FP8X4),
                 lhsT_scale=tiles["w_scales", m][:, feats],
-                rhs=codes[:].bitcast(FP8X4),
-                rhs_scale=scales[:],
+                rhs=tiles[operand + "_codes", k][:].bitcast(FP8X4),
+                rhs_scale=tiles[operand + "_scales", k][:],
                 start=True,
                 stop=True,
             )
+
+        def quantise(operand, k):
+            codes = quant.tile([P, UNIT_ROWS], U32, tag=operand + "_codes", align_bytes=64)
+            scales = quant.tile([P, UNIT_ROWS], U8, tag=operand + "_scales", align_bytes=64)
+            nc.vector.quantize_mx(out=codes[:].bitcast(FP8X4), scales=scales[:], in_=tiles[operand + "_grp", k][:])
+            tiles[operand + "_codes", k] = codes
+            tiles[operand + "_scales", k] = scales
 
         def unit_rows(dram, k):
             first = (k % UNITS) * UNIT_ROWS
@@ -143,73 +155,50 @@ def tile_variableselectionnetwork_pb_t_kernel(
             tiles["sel_u", k] = sel_u
 
         def hv_transpose(k, half):
-            hv_words = tiles["hv_u", k][:].bitcast(F32)
             if half == 0:
-                hv_grp = quant.tile([P, UNIT_ROWS * PACK], BF16, tag="hv_grp", align_bytes=64)
-            else:
-                hv_grp = tiles["hv_grp", k]
-            hv_grp_words = hv_grp[:].bitcast(F32).rearrange("p (b u) -> p b u", u=2)
-            if True:
-                hv_t = psum.tile([P, 2, 2 * P], F32, tag="to_scalar")
-                for u in range(2):
-                    for j in range(2):
-                        i = 2 * half + j
-                        nc.tensor.transpose(
-                            hv_t[:, u, j * P : (j + 1) * P],
-                            hv_words[:, i * 2 * P + u * P : i * 2 * P + (u + 1) * P],
-                            ident_f[:],
-                        )
-                nc.scalar.copy(
-                    out=hv_grp_words[:, half * 2 * P : (half + 1) * 2 * P, :],
-                    in_=hv_t[:].rearrange("p u b -> p b u"),
+                tiles["hv_grp", k] = quant.tile(
+                    [P, UNIT_ROWS * PACK], BF16, tag="hv_grp", name="hv_grp", align_bytes=64
                 )
-            tiles["hv_grp", k] = hv_grp
-
-        def hv_quantise(k):
-            codes = quant.tile([P, UNIT_ROWS], U32, tag="hv_codes", align_bytes=64)
-            scales = quant.tile([P, UNIT_ROWS], U8, tag="hv_scales", align_bytes=64)
-            nc.vector.quantize_mx(out=codes[:].bitcast(FP8X4), scales=scales[:], in_=tiles["hv_grp", k][:])
-            tiles["hv_codes", k] = codes
-            tiles["hv_scales", k] = scales
+            hv_words = tiles["hv_u", k][:].bitcast(F32)
+            hv_grp_words = tiles["hv_grp", k][:].bitcast(F32).rearrange("p (b u) -> p b u", u=PACK // PAIR)
+            hv_t = psum.tile([P, PACK // PAIR, 2 * P], F32, tag="to_scalar")
+            for u in range(PACK // PAIR):
+                for j in range(2):
+                    first_word = (2 * half + j) * (D // PAIR) + u * P
+                    nc.tensor.transpose(
+                        hv_t[:, u, j * P : (j + 1) * P], hv_words[:, first_word : first_word + P], ident_f[:]
+                    )
+            nc.scalar.copy(
+                out=hv_grp_words[:, half * 2 * P : (half + 1) * 2 * P, :], in_=hv_t[:].rearrange("p u b -> p b u")
+            )
 
         def first_layer(k):
             n = k // UNITS
             planes = quant.tile([P, CHUNKS, UNIT_ROWS], BF16, tag="e1_planes")
             for c in range(CHUNKS):
                 e1_ps = psum.tile([P, UNIT_ROWS], F32, tag="to_scalar")
-                mx_pass(e1_ps[:], 3 * n, c, tiles["hv_codes", k], tiles["hv_scales", k])
+                mx_pass(e1_ps[:], MATRICES * n, c, "hv", k)
                 nc.scalar.activation(
                     out=planes[:, c, :], in_=e1_ps[:], func=ACT.Identity, bias=bias_cols[:, 0, n, c : c + 1], scale=1.0
                 )
             tiles["e1_planes", k] = planes
 
         def e1_regroup(k):
-            grouped = quant.tile([P, UNIT_ROWS, PACK], BF16, tag="e1_grp", align_bytes=64)
+            grouped = quant.tile([P, UNIT_ROWS * PACK], BF16, tag="e1_grp", align_bytes=64)
             nc.vector.tensor_copy(
-                out=grouped[:].rearrange("p (b i) t -> p b t i", i=4),
-                in_=tiles["e1_planes", k][:].rearrange("p t (b i) -> p b t i", i=4),
+                out=grouped[:].rearrange("p (b i t) -> p b t i", i=RUN, t=PACK),
+                in_=tiles["e1_planes", k][:].rearrange("p t (b i) -> p b t i", i=RUN),
             )
             tiles["e1_grp", k] = grouped
-
-        def e1_quantise(k):
-            codes = quant.tile([P, UNIT_ROWS], U32, tag="e1_codes", align_bytes=64)
-            scales = quant.tile([P, UNIT_ROWS], U8, tag="e1_scales", align_bytes=64)
-            nc.vector.quantize_mx(
-                out=codes[:].bitcast(FP8X4),
-                scales=scales[:],
-                in_=tiles["e1_grp", k][:].rearrange("p b t -> p (b t)"),
-            )
-            tiles["e1_codes", k] = codes
-            tiles["e1_scales", k] = scales
 
         def gate_layers(k):
             n = k // UNITS
             gv_t = gate.tile([P, CHUNKS, UNIT_ROWS], F32, tag="gv_t")
             for c in range(CHUNKS):
                 g4_ps = psum.tile([P, UNIT_ROWS], F32, tag="to_scalar")
-                mx_pass(g4_ps[:], 3 * n + 1, c, tiles["e1_codes", k], tiles["e1_scales", k])
+                mx_pass(g4_ps[:], MATRICES * n + 1, c, "e1", k)
                 g5_ps = psum.tile([P, UNIT_ROWS], F32, tag="to_vector", bufs=3)
-                mx_pass(g5_ps[:], 3 * n + 2, c, tiles["e1_codes", k], tiles["e1_scales", k])
+                mx_pass(g5_ps[:], MATRICES * n + 2, c, "e1", k)
                 sig = gate.tile([P, UNIT_ROWS], F32, tag="sig", bufs=3)
                 nc.scalar.activation(
                     out=sig[:], in_=g4_ps[:], func=ACT.Sigmoid, bias=bias_cols[:, 1, n, c : c + 1], scale=1.0
@@ -268,7 +257,7 @@ def tile_variableselectionnetwork_pb_t_kernel(
             yv = gate.tile([P, UNIT_TILES, D], F32, tag="yv")
             for i in range(UNIT_TILES):
                 r = tiles["r%d" % i, k]
-                squares = norm.tile([P, D], BF16, tag="squares", bufs=4)
+                squares = norm.tile([P, D], BF16, tag="squares", bufs=UNIT_TILES)
                 nc.scalar.activation(
                     out=squares[:],
                     in_=r[:],
@@ -278,8 +267,12 @@ def tile_variableselectionnetwork_pb_t_kernel(
                     accum_out=sq_sum[:, i : i + 1],
                 )
                 nc.vector.scalar_tensor_tensor(
-                    out=yv[:, i, :], in0=r[:], scalar=neg_mean[:, i : i + 1], in1=tiles["gain_shift", n][:, 0, :],
-                    op0=ALU.add, op1=ALU.mult,
+                    out=yv[:, i, :],
+                    in0=r[:],
+                    scalar=neg_mean[:, i : i + 1],
+                    in1=tiles["gain_shift", n][:, 0, :],
+                    op0=ALU.add,
+                    op1=ALU.mult,
                 )
             tiles["yv", k] = yv
             var_eps = stat.tile([P, UNIT_TILES], F32, tag="var_eps")
@@ -288,56 +281,56 @@ def tile_variableselectionnetwork_pb_t_kernel(
             nc.gpsimd.tensor_tensor(out=rstd[:], in0=var_eps[:], in1=neg_half[:], op=ALU.pow)
             tiles["rstd", k] = rstd
 
-        def unit_acc(k):
-            first = (k % UNITS) * UNIT_TILES
-            return acc[:, first : first + UNIT_TILES, :]
-
         def scale_shift(k):
-            n = k // UNITS
             yv = tiles["yv", k]
             for i in range(UNIT_TILES):
                 nc.vector.scalar_tensor_tensor(
                     out=yv[:, i, :],
                     in0=yv[:, i, :],
                     scalar=tiles["rstd", k][:, i : i + 1],
-                    in1=tiles["gain_shift", n][:, 1, :],
+                    in1=tiles["gain_shift", k // UNITS][:, 1, :],
                     op0=ALU.mult,
                     op1=ALU.add,
                 )
 
         def weigh(k):
             yv = tiles["yv", k]
+            sel_u = tiles["sel_u", k]
             if k // UNITS == 0:
                 for i in range(UNIT_TILES):
                     nc.gpsimd.tensor_tensor(
-                        out=unit_acc(k)[:, i, :], in0=yv[:, i, :], in1=tiles["sel_u", k][:, i, :], op=ALU.mult
+                        out=acc[:, k * UNIT_TILES + i, :], in0=yv[:, i, :], in1=sel_u[:, i, :], op=ALU.mult
                     )
             else:
-                nc.vector.tensor_tensor(out=yv[:], in0=yv[:], in1=tiles["sel_u", k][:], op=ALU.mult)
+                nc.vector.tensor_tensor(out=yv[:], in0=yv[:], in1=sel_u[:], op=ALU.mult)
 
-        def accumulate(k, first_tile):
+        def accumulate(k, half):
             adder = nc.vector if k == TOTAL - 1 else nc.gpsimd
-            for i in range(first_tile, first_tile + UNIT_TILES // 2):
+            for i in range(half * UNIT_TILES // 2, (half + 1) * UNIT_TILES // 2):
                 tile_no = (k % UNITS) * UNIT_TILES + i
+                total = acc[:, tile_no, :]
                 if k // UNITS > 0:
-                    adder.tensor_tensor(
-                        out=acc[:, tile_no, :], in0=acc[:, tile_no, :], in1=tiles["yv", k][:, i, :], op=ALU.add
-                    )
+                    adder.tensor_tensor(out=total, in0=total, in1=tiles["yv", k][:, i, :], op=ALU.add)
                 if k // UNITS == VARS - 1:
-                    nc.sync.dma_start(out=out[tile_no * P : (tile_no + 1) * P, :], in_=acc[:, tile_no, :])
+                    nc.sync.dma_start(out=out[tile_no * P : (tile_no + 1) * P, :], in_=total)
 
-        for step in range(-4, TOTAL + 1):
-            if live(step + 4):
-                load_hv(step + 4)
+        def live(k):
+            return 0 <= k < TOTAL
+
+        def weights_loaded_in(s):
+            first = WEIGHTS_A_STEP * (s + LEAD) - 1
+            return [m for m in range(first, first + WEIGHTS_A_STEP) if 0 <= m < WEIGHTS]
+
+        for step in range(-LEAD, TOTAL + 1):
+            if live(step + LEAD):
+                load_hv(step + LEAD)
             if live(step + 1):
                 load_x_sel(step + 1)
-            for m in (2 * step + 7, 2 * step + 8):
-                if live(m):
-                    weight_load(m)
+            for m in weights_loaded_in(step):
+                weight_load(m)
 
-            for m in (2 * step + 3, 2 * step + 4):
-                if live(m):
-                    weight_quantise(m)
+            for m in weights_loaded_in(step - 2):
+                weight_quantise(m)
             if live(step):
                 gate_layers(step)
             if live(step + 1):
@@ -359,15 +352,14 @@ def tile_variableselectionnetwork_pb_t_kernel(
             if live(step - 1):
                 weigh(step - 1)
             if live(step + 1):
-                e1_quantise(step + 1)
+                quantise("e1", step + 1)
             if live(step - 1):
                 accumulate(step - 1, 0)
             if live(step):
                 centre(step)
             if live(step - 1):
-                accumulate(step - 1, UNIT_TILES // 2)
+                accumulate(step - 1, 1)
             if live(step + 2):
-                hv_quantise(step + 2)
-            for m in (2 * step + 5, 2 * step + 6):
-                if live(m):
-                    weight_regroup(m)
+                quantise("hv", step + 2)
+            for m in weights_loaded_in(step - 1):
+                weight_regroup(m)

from contextlib import ExitStack

import concourse.mybir as mybir
from concourse.masks import make_identity

F32 = mybir.dt.float32
BF16 = mybir.dt.bfloat16
U32 = mybir.dt.uint32
U8 = mybir.dt.uint8
FP8X4 = mybir.dt.float8_e4m3fn_x4
ALU = mybir.AluOpType
ACT = mybir.ActivationFunctionType

P = 128
PACK = 4
PAIR = 2
BATCH = 1536
VARS = 4
D = 512
CHUNKS = D // P
UNIT_ROWS = 512
UNIT_TILES = UNIT_ROWS // P
UNITS = BATCH // UNIT_ROWS
TOTAL = VARS * UNITS
MATRICES = 3
WEIGHTS = MATRICES * VARS
WEIGHTS_A_STEP = 2
LEAD = 4
RUN = 4
VECTOR_COLUMNS = 320
EPS = 1e-5

FLOPS = MATRICES * VARS * 2 * BATCH * D * D


def tile_variableselectionnetwork_pb_t_kernel(
    tc, hv, x, sel_w, vW1, vb1, vW4, vb4, vW5, vb5, vlng, vlnb, out
):
    nc = tc.nc
    with ExitStack() as ctx:
        ctx.enter_context(tc.manual_schedule())
        const = ctx.enter_context(tc.tile_pool(name="const", bufs=1))
        wstage = ctx.enter_context(tc.tile_pool(name="wstage", bufs=WEIGHTS_A_STEP))
        wquant = ctx.enter_context(tc.tile_pool(name="wquant", bufs=VARS))
        loads = ctx.enter_context(tc.tile_pool(name="loads", bufs=4))
        quant = ctx.enter_context(tc.tile_pool(name="quant", bufs=2))
        gate = ctx.enter_context(tc.tile_pool(name="gate", bufs=2))
        norm = ctx.enter_context(tc.tile_pool(name="norm", bufs=2 * UNIT_TILES))
        stat = ctx.enter_context(tc.tile_pool(name="stat", bufs=3))
        psum = ctx.enter_context(tc.psum_pool(name="psum", bufs=4))

        ident_f = const.tile([P, P], F32)
        make_identity(nc, ident_f[:])
        ident_b = const.tile([P, P], BF16)
        make_identity(nc, ident_b[:])
        neg_half = const.tile([P, UNIT_TILES], F32)
        nc.vector.memset(neg_half[:], -0.5)
        warm = const.tile([P, UNIT_TILES], F32)
        nc.scalar.activation(out=warm[:], in_=neg_half[:], func=ACT.Sigmoid)

        bias_rows = const.tile([P, P], BF16)
        nc.vector.memset(bias_rows[:], 0.0)
        for k, vec in enumerate((vb1, vb4, vb5)):
            nc.scalar.dma_start(
                out=bias_rows[k * VARS * CHUNKS : (k + 1) * VARS * CHUNKS, :],
                in_=vec.rearrange("n (c m) -> (n c) m", m=P),
            )
        gs_rows = const.tile([P, D], BF16)
        nc.vector.memset(gs_rows[:], 0.0)
        nc.scalar.dma_start(out=gs_rows[0:VARS, :], in_=vlng)
        nc.scalar.dma_start(out=gs_rows[VARS : 2 * VARS, :], in_=vlnb)

        bias_ps = psum.tile([P, P], BF16, tag="to_scalar")
        nc.tensor.transpose(bias_ps[:], bias_rows[:], ident_b[:])
        bias_cols = const.tile([P, MATRICES, VARS, CHUNKS], F32)
        nc.scalar.copy(
            out=bias_cols[:].rearrange("p k n c -> p (k n c)"), in_=bias_ps[:, 0 : MATRICES * VARS * CHUNKS]
        )

        acc = const.tile([P, BATCH // P, D], F32)

        tiles = {}

        def weight_load(m):
            n = m // MATRICES
            raw = wstage.tile([P, PACK, D], BF16, tag="w_raw", bufs=2 * WEIGHTS_A_STEP)
            if m % MATRICES == 0:
                nc.sync.dma_start(
                    out=raw[:].rearrange("p (u e) c -> p u e c", e=PAIR),
                    in_=vW1[n].rearrange("(u p e) c -> p u e c", p=P, e=PAIR),
                )
            else:
                w = vW4 if m % MATRICES == 1 else vW5
                nc.sync.dma_start(out=raw[:], in_=w[n].rearrange("(t p) c -> p t c", p=P))
            tiles["w_raw", m] = raw

        def weight_regroup(m):
            raw = tiles["w_raw", m]
            grouped = wstage.tile([P, D, PACK], BF16, tag="w_grp", align_bytes=64)
            nc.vector.tensor_copy(
                out=grouped[:, 0:VECTOR_COLUMNS, :].rearrange("p (c i) t -> p c t i", i=RUN),
                in_=raw[:, :, 0:VECTOR_COLUMNS].rearrange("p t (c i) -> p c t i", i=RUN),
            )
            nc.scalar.copy(
                out=grouped[:, VECTOR_COLUMNS:D, :].rearrange("p (c i) t -> p c t i", i=RUN),
                in_=raw[:, :, VECTOR_COLUMNS:D].rearrange("p t (c i) -> p c t i", i=RUN),
            )
            tiles["w_grp", m] = grouped

        def weight_quantise(m):
            codes = wquant.tile([P, D], U32, tag="w_codes%d" % (m % MATRICES), align_bytes=64)
            scales = wquant.tile([P, D], U8, tag="w_scales%d" % (m % MATRICES), align_bytes=64)
            nc.vector.quantize_mx(
                out=codes[:].bitcast(FP8X4),
                scales=scales[:],
                in_=tiles["w_grp", m][:].rearrange("p c t -> p (c t)"),
            )
            tiles["w_codes", m] = codes
            tiles["w_scales", m] = scales

        def mx_pass(out_ps, m, c, operand, k):
            feats = slice(c * P, (c + 1) * P)
            nc.tensor.matmul_mx(
                out=out_ps,
                lhsT=tiles["w_codes", m][:, feats].bitcast(FP8X4),
                lhsT_scale=tiles["w_scales", m][:, feats],
                rhs=tiles[operand + "_codes", k][:].bitcast(FP8X4),
                rhs_scale=tiles[operand + "_scales", k][:],
                start=True,
                stop=True,
            )

        def quantise(operand, k):
            codes = quant.tile([P, UNIT_ROWS], U32, tag=operand + "_codes", align_bytes=64)
            scales = quant.tile([P, UNIT_ROWS], U8, tag=operand + "_scales", align_bytes=64)
            nc.vector.quantize_mx(out=codes[:].bitcast(FP8X4), scales=scales[:], in_=tiles[operand + "_grp", k][:])
            tiles[operand + "_codes", k] = codes
            tiles[operand + "_scales", k] = scales

        def unit_rows(dram, k):
            first = (k % UNITS) * UNIT_ROWS
            return dram[first : first + UNIT_ROWS, k // UNITS, :].rearrange("(i p) d -> p i d", p=P)

        def load_hv(k):
            hv_u = loads.tile([P, UNIT_TILES * D], BF16, tag="hv_u")
            nc.sync.dma_start(out=hv_u[:].rearrange("p (i d) -> p i d", i=UNIT_TILES), in_=unit_rows(hv, k))
            tiles["hv_u", k] = hv_u

        def load_x_sel(k):
            x_u = loads.tile([P, UNIT_TILES, D], BF16, tag="x_u", bufs=3)
            nc.sync.dma_start(out=x_u[:], in_=unit_rows(x, k))
            sel_u = loads.tile([P, UNIT_TILES, D], BF16, tag="sel_u")
            nc.sync.dma_start(out=sel_u[:], in_=unit_rows(sel_w, k))
            tiles["x_u", k] = x_u
            tiles["sel_u", k] = sel_u

        def hv_transpose(k, half):
            if half == 0:
                tiles["hv_grp", k] = quant.tile(
                    [P, UNIT_ROWS * PACK], BF16, tag="hv_grp", name="hv_grp", align_bytes=64
                )
            hv_words = tiles["hv_u", k][:].bitcast(F32)
            hv_grp_words = tiles["hv_grp", k][:].bitcast(F32).rearrange("p (b u) -> p b u", u=PACK // PAIR)
            hv_t = psum.tile([P, PACK // PAIR, 2 * P], F32, tag="to_scalar")
            for u in range(PACK // PAIR):
                for j in range(2):
                    first_word = (2 * half + j) * (D // PAIR) + u * P
                    nc.tensor.transpose(
                        hv_t[:, u, j * P : (j + 1) * P], hv_words[:, first_word : first_word + P], ident_f[:]
                    )
            nc.scalar.copy(
                out=hv_grp_words[:, half * 2 * P : (half + 1) * 2 * P, :], in_=hv_t[:].rearrange("p u b -> p b u")
            )

        def first_layer(k):
            n = k // UNITS
            planes = quant.tile([P, CHUNKS, UNIT_ROWS], BF16, tag="e1_planes")
            for c in range(CHUNKS):
                e1_ps = psum.tile([P, UNIT_ROWS], F32, tag="to_scalar")
                mx_pass(e1_ps[:], MATRICES * n, c, "hv", k)
                nc.scalar.activation(
                    out=planes[:, c, :], in_=e1_ps[:], func=ACT.Identity, bias=bias_cols[:, 0, n, c : c + 1], scale=1.0
                )
            tiles["e1_planes", k] = planes

        def e1_regroup(k):
            grouped = quant.tile([P, UNIT_ROWS * PACK], BF16, tag="e1_grp", align_bytes=64)
            nc.vector.tensor_copy(
                out=grouped[:].rearrange("p (b i t) -> p b t i", i=RUN, t=PACK),
                in_=tiles["e1_planes", k][:].rearrange("p t (b i) -> p b t i", i=RUN),
            )
            tiles["e1_grp", k] = grouped

        def gate_layers(k):
            n = k // UNITS
            gv_t = gate.tile([P, CHUNKS, UNIT_ROWS], F32, tag="gv_t")
            for c in range(CHUNKS):
                g4_ps = psum.tile([P, UNIT_ROWS], F32, tag="to_scalar")
                mx_pass(g4_ps[:], MATRICES * n + 1, c, "e1", k)
                g5_ps = psum.tile([P, UNIT_ROWS], F32, tag="to_vector", bufs=3)
                mx_pass(g5_ps[:], MATRICES * n + 2, c, "e1", k)
                sig = gate.tile([P, UNIT_ROWS], F32, tag="sig", bufs=3)
                nc.scalar.activation(
                    out=sig[:], in_=g4_ps[:], func=ACT.Sigmoid, bias=bias_cols[:, 1, n, c : c + 1], scale=1.0
                )
                nc.vector.scalar_tensor_tensor(
                    out=gv_t[:, c, :],
                    in0=g5_ps[:],
                    scalar=bias_cols[:, 2, n, c : c + 1],
                    in1=sig[:],
                    op0=ALU.add,
                    op1=ALU.mult,
                )
            tiles["gv_t", k] = gv_t

        def residual(k):
            row_sum = stat.tile([P, UNIT_TILES], F32, tag="row_sum")
            for i in range(UNIT_TILES):
                r_ps = psum.tile([P, D], F32, tag="to_scalar")
                nc.tensor.matmul(out=r_ps[:], lhsT=ident_b[:], rhs=tiles["x_u", k][:, i, :], start=True, stop=False)
                for c in range(CHUNKS):
                    nc.tensor.matmul(
                        out=r_ps[:, c * P : (c + 1) * P],
                        lhsT=tiles["gv_t", k][:, c, i * P : (i + 1) * P],
                        rhs=ident_f[:],
                        is_transpose=True,
                        start=False,
                        stop=(c == CHUNKS - 1),
                    )
                r = norm.tile([P, D], F32, tag="r")
                nc.scalar.activation(out=r[:], in_=r_ps[:], func=ACT.Identity, accum_out=row_sum[:, i : i + 1])
                tiles["r%d" % i, k] = r
            tiles["row_sum", k] = row_sum

        def mean(k):
            neg_mean = stat.tile([P, UNIT_TILES], F32, tag="neg_mean")
            nc.scalar.mul(out=neg_mean[:], in_=tiles["row_sum", k][:], mul=-1.0 / D)
            tiles["neg_mean", k] = neg_mean

        def spread_gain_shift(n):
            gs_ps = psum.tile([P, 2, D], BF16, tag="gain_shift", bufs=1)
            for v in range(2):
                row = v * VARS + n
                nc.tensor.matmul(
                    out=gs_ps[:, v, :],
                    lhsT=ident_b[:, row : row + 1].to_broadcast([P, P]),
                    rhs=gs_rows[:],
                    start=True,
                    stop=True,
                )
            tiles["gain_shift", n] = gs_ps

        def centre(k):
            n = k // UNITS
            neg_mean = tiles["neg_mean", k]
            sq_sum = stat.tile([P, UNIT_TILES], F32, tag="sq_sum")
            yv = gate.tile([P, UNIT_TILES, D], F32, tag="yv")
            for i in range(UNIT_TILES):
                r = tiles["r%d" % i, k]
                squares = norm.tile([P, D], BF16, tag="squares", bufs=UNIT_TILES)
                nc.scalar.activation(
                    out=squares[:],
                    in_=r[:],
                    func=ACT.Square,
                    bias=neg_mean[:, i : i + 1],
                    scale=1.0,
                    accum_out=sq_sum[:, i : i + 1],
                )
                nc.vector.scalar_tensor_tensor(
                    out=yv[:, i, :],
                    in0=r[:],
                    scalar=neg_mean[:, i : i + 1],
                    in1=tiles["gain_shift", n][:, 0, :],
                    op0=ALU.add,
                    op1=ALU.mult,
                )
            tiles["yv", k] = yv
            var_eps = stat.tile([P, UNIT_TILES], F32, tag="var_eps")
            nc.scalar.activation(out=var_eps[:], in_=sq_sum[:], func=ACT.Copy, bias=EPS, scale=1.0 / D)
            rstd = stat.tile([P, UNIT_TILES], F32, tag="rstd")
            nc.gpsimd.tensor_tensor(out=rstd[:], in0=var_eps[:], in1=neg_half[:], op=ALU.pow)
            tiles["rstd", k] = rstd

        def scale_shift(k):
            yv = tiles["yv", k]
            for i in range(UNIT_TILES):
                nc.vector.scalar_tensor_tensor(
                    out=yv[:, i, :],
                    in0=yv[:, i, :],
                    scalar=tiles["rstd", k][:, i : i + 1],
                    in1=tiles["gain_shift", k // UNITS][:, 1, :],
                    op0=ALU.mult,
                    op1=ALU.add,
                )

        def weigh(k):
            yv = tiles["yv", k]
            sel_u = tiles["sel_u", k]
            if k // UNITS == 0:
                for i in range(UNIT_TILES):
                    nc.gpsimd.tensor_tensor(
                        out=acc[:, k * UNIT_TILES + i, :], in0=yv[:, i, :], in1=sel_u[:, i, :], op=ALU.mult
                    )
            else:
                nc.vector.tensor_tensor(out=yv[:], in0=yv[:], in1=sel_u[:], op=ALU.mult)

        def accumulate(k, half):
            adder = nc.vector if k == TOTAL - 1 else nc.gpsimd
            for i in range(half * UNIT_TILES // 2, (half + 1) * UNIT_TILES // 2):
                tile_no = (k % UNITS) * UNIT_TILES + i
                total = acc[:, tile_no, :]
                if k // UNITS > 0:
                    adder.tensor_tensor(out=total, in0=total, in1=tiles["yv", k][:, i, :], op=ALU.add)
                if k // UNITS == VARS - 1:
                    nc.sync.dma_start(out=out[tile_no * P : (tile_no + 1) * P, :], in_=total)

        def live(k):
            return 0 <= k < TOTAL

        def weights_loaded_in(s):
            first = WEIGHTS_A_STEP * (s + LEAD) - 1
            return [m for m in range(first, first + WEIGHTS_A_STEP) if 0 <= m < WEIGHTS]

        for step in range(-LEAD, TOTAL + 1):
            if live(step + LEAD):
                load_hv(step + LEAD)
            if live(step + 1):
                load_x_sel(step + 1)
            for m in weights_loaded_in(step):
                weight_load(m)

            for m in weights_loaded_in(step - 2):
                weight_quantise(m)
            if live(step):
                gate_layers(step)
            if live(step + 1):
                first_layer(step + 1)
            if live(step):
                residual(step)
            if live(step + 2):
                hv_transpose(step + 2, 0)
            if live(step):
                mean(step)
            if live(step + 2):
                hv_transpose(step + 2, 1)
            if live(step - 1):
                scale_shift(step - 1)
            if live(step) and step % UNITS == 0:
                spread_gain_shift(step // UNITS)
            if live(step + 1):
                e1_regroup(step + 1)
            if live(step - 1):
                weigh(step - 1)
            if live(step + 1):
                quantise("e1", step + 1)
            if live(step - 1):
                accumulate(step - 1, 0)
            if live(step):
                centre(step)
            if live(step - 1):
                accumulate(step - 1, 1)
            if live(step + 2):
                quantise("hv", step + 2)
            for m in weights_loaded_in(step - 1):
                weight_regroup(m)
